import numpy as np
import ml_dtypes


def mxq(x, axis, fmt="e4m3"):
    dtype, down = {"e4m3": (ml_dtypes.float8_e4m3fn, 7), "e5m2": (ml_dtypes.float8_e5m2, 14)}[fmt]
    v = np.moveaxis(np.asarray(x, np.float32).astype(ml_dtypes.bfloat16).astype(np.float64), axis, -1)
    blocks = v.reshape(v.shape[:-1] + (-1, 32))
    amax = np.abs(blocks).max(-1, keepdims=True)
    byte = np.maximum(np.where(amax > 0, np.frexp(amax)[1] - 1 + 127, 0) - down, 1)
    scale = np.exp2(byte - 127.0)
    codes = (blocks / scale).astype(np.float32).astype(dtype).astype(np.float64)
    return np.moveaxis((codes * scale).reshape(v.shape), -1, axis)


WIDE = False


def mx_kscale(k):
    if not WIDE:
        return np.ones(k)
    levels = np.array([10, -10, 5, -5, 0])
    a = np.random.permutation(np.resize(levels, k // 512 * 4)).reshape(k // 512, 4)
    idx = np.arange(k)
    return np.exp2(a[idx // 512, idx % 128 // 32])


BF16 = ml_dtypes.bfloat16


def bf(x):
    return np.asarray(x, np.float32).astype(BF16)


def f64(x):
    return np.asarray(x).astype(np.float64)


B, T, C, H, D, R = 1, 1024, 2048, 16, 128, 512
EPS = 1e-6
THETA = 10000.0


def rmsnorm(v, w):
    var = np.mean(v * v, axis=-1, keepdims=True)
    return v * (1.0 / np.sqrt(var + EPS)) * w


def rope(v, cos, sin):
    re, im = v[..., 0::2], v[..., 1::2]
    c, s = cos[None, :, None, :], sin[None, :, None, :]
    return np.stack([re * c - im * s, re * s + im * c], axis=-1).reshape(v.shape)


def setup_inputs():
    s = mx_kscale(C)
    ang = np.outer(np.arange(T), 1.0 / THETA ** (np.arange(0, D, 2) / D))
    return {"x": bf(np.random.standard_normal((B, T, C)) * s),
            "wq": bf(np.random.standard_normal((H * D, C)) / np.sqrt(C) / s[None, :]),
            "q_norm_w": bf(1.0 + 0.1 * np.random.standard_normal(D)),
            "freqs_cos": bf(np.cos(ang)), "freqs_sin": bf(np.sin(ang))}


def reference(x, wq, q_norm_w, freqs_cos, freqs_sin):
    xq = (mxq(f64(x), 2, "e4m3") @ mxq(f64(wq), 1, "e4m3").T).reshape(B, T, H, D)
    return rope(rmsnorm(xq, f64(q_norm_w)), f64(freqs_cos), f64(freqs_sin))

@@ -1,0 +1,224 @@
+from contextlib import ExitStack
+
+import concourse.mybir as mybir
+from concourse.masks import make_identity
+
+FP8X4 = mybir.dt.float8_e4m3fn_x4
+BF16 = mybir.dt.bfloat16
+F32 = mybir.dt.float32
+U32 = mybir.dt.uint32
+U8 = mybir.dt.uint8
+ACT = mybir.ActivationFunctionType
+ALU = mybir.AluOpType
+
+P = 128
+TOKENS = 1024
+K = 2048
+HEADS = 16
+HEAD_DIM = 128
+PAIRS = HEAD_DIM // 2
+EPS = 1e-6
+
+K_PASS = 4 * P
+PASSES = K // K_PASS
+PASS_WORDS = K_PASS // 2
+TOKEN_TILES = TOKENS // P
+BLOCK_HEADS = 4
+BLOCK_COLS = BLOCK_HEADS * HEAD_DIM
+BLOCKS = HEADS // BLOCK_HEADS
+GROUPS = BLOCKS * TOKEN_TILES
+UNIT_COLS = 512
+
+W_LEAD = 3
+X_LEAD = 2
+
+FLOPS = 2 * TOKENS * K * HEADS * HEAD_DIM
+
+
+def tile_mla_pb_kernel(tc, x, wq, q_norm_w, freqs_cos, freqs_sin, out):
+    nc = tc.nc
+    x_view = x.rearrange("b (p t) k -> p (b t) k", t=TOKEN_TILES)
+    cos_view = freqs_cos.rearrange("(p t) j -> p t j", t=TOKEN_TILES)
+    sin_view = freqs_sin.rearrange("(p t) j -> p t j", t=TOKEN_TILES)
+    out_view = out.rearrange("b (p t) h d -> p (b t) (h d)", t=TOKEN_TILES)
+    wq_view = wq.rearrange("(h p) k -> p h k", p=P)
+
+    with ExitStack() as ctx:
+        const = ctx.enter_context(tc.tile_pool(name="const", bufs=1))
+        raw = ctx.enter_context(tc.tile_pool(name="raw", bufs=1))
+        keep = ctx.enter_context(tc.tile_pool(name="keep", bufs=1))
+        stage = ctx.enter_context(tc.tile_pool(name="stage", bufs=4))
+        work = ctx.enter_context(tc.tile_pool(name="work", bufs=3))
+        small = ctx.enter_context(tc.tile_pool(name="small", bufs=4))
+        tpsum = ctx.enter_context(tc.psum_pool(name="tpsum", bufs=4))
+        mpsum = ctx.enter_context(tc.psum_pool(name="mpsum", bufs=4))
+        ctx.enter_context(tc.manual_schedule())
+
+        w_raw = [raw.tile([P, 2, K], BF16, name="w_raw%d" % i) for i in range(HEADS // 2)]
+        x_raw = [raw.tile([P, 2, K], BF16, name="x_raw%d" % i) for i in range(TOKEN_TILES // 2)]
+
+        def load_w(i):
+            nc.sync.dma_start(out=w_raw[i][:], in_=wq_view[:, 2 * i : 2 * i + 2, :])
+
+        def load_x(i):
+            nc.sync.dma_start(out=x_raw[i][:], in_=x_view[:, 2 * i : 2 * i + 2, :])
+
+        for i in range(BLOCK_HEADS // 2):
+            load_w(i)
+        for i in range(TOKEN_TILES // 2):
+            load_x(i)
+        for i in range(BLOCK_HEADS // 2, HEADS // 2):
+            load_w(i)
+
+        cos_sb = const.tile([P, TOKEN_TILES, PAIRS], BF16, name="cos_sb")
+        sin_sb = const.tile([P, TOKEN_TILES, PAIRS], BF16, name="sin_sb")
+        gain_sb = const.tile([P, PAIRS, 2], BF16, name="gain_sb")
+        nc.scalar.dma_start(out=cos_sb[:], in_=cos_view)
+        nc.scalar.dma_start(out=sin_sb[:], in_=sin_view)
+        nc.scalar.dma_start(
+            out=gain_sb[:].rearrange("p j e -> p (j e)"), in_=q_norm_w.partition_broadcast(P)
+        )
+
+        ident = const.tile([P, P], F32, name="ident")
+        make_identity(nc, ident[:])
+        eps_sb = const.tile([P, 1], F32, name="eps_sb")
+        nc.vector.memset(eps_sb[:], EPS)
+        warm = const.tile([P, 1], F32, name="warm")
+        nc.scalar.activation(out=warm[:], in_=eps_sb[:], func=ACT.Sqrt)
+
+        even_table = const.tile([P, TOKEN_TILES, PAIRS, 2], F32, name="even_table")
+        odd_table = const.tile([P, TOKEN_TILES, PAIRS, 2], F32, name="odd_table")
+        table_shape = [P, TOKEN_TILES, PAIRS]
+        gain_even = gain_sb[:, :, 0].unsqueeze(1).to_broadcast(table_shape)
+        gain_odd = gain_sb[:, :, 1].unsqueeze(1).to_broadcast(table_shape)
+        nc.vector.tensor_tensor(out=even_table[:, :, :, 0], in0=cos_sb[:], in1=gain_even, op=ALU.mult)
+        nc.vector.tensor_tensor(out=even_table[:, :, :, 1], in0=sin_sb[:], in1=gain_even, op=ALU.mult)
+        nc.vector.scalar_tensor_tensor(
+            out=odd_table[:, :, :, 0], in0=sin_sb[:], scalar=-1.0, in1=gain_odd, op0=ALU.mult, op1=ALU.mult
+        )
+        nc.vector.tensor_tensor(out=odd_table[:, :, :, 1], in0=cos_sb[:], in1=gain_odd, op=ALU.mult)
+
+        x_codes = [keep.tile([P, UNIT_COLS], U32, name="x_codes%d" % t, align_bytes=64) for t in range(TOKEN_TILES)]
+        x_scales = [keep.tile([P, UNIT_COLS], U8, name="x_scales%d" % t, align_bytes=64) for t in range(TOKEN_TILES)]
+        w_codes = [keep.tile([P, UNIT_COLS], U32, name="w_codes%d" % i, align_bytes=64) for i in range(BLOCKS * PASSES)]
+        w_scales = [keep.tile([P, UNIT_COLS], U8, name="w_scales%d" % i, align_bytes=64) for i in range(BLOCKS * PASSES)]
+
+        def pass_words(rows, g):
+            return rows.bitcast(F32)[:, g * PASS_WORDS : (g + 1) * PASS_WORDS]
+
+        def x_unit(t):
+            rows = x_raw[t // 2][:, t % 2, :]
+            return [pass_words(rows, g) for g in range(PASSES)], x_codes[t], x_scales[t]
+
+        def w_unit(b, g):
+            heads = [BLOCK_HEADS * b + a for a in range(BLOCK_HEADS)]
+            sources = [pass_words(w_raw[h // 2][:, h % 2, :], g) for h in heads]
+            return sources, w_codes[b * PASSES + g], w_scales[b * PASSES + g]
+
+        def units_of_slot(s):
+            units = []
+            block, place = divmod(s + W_LEAD, TOKEN_TILES)
+            if block < BLOCKS and place < 2:
+                units.append(w_unit(block, 2 * place))
+                units.append(w_unit(block, 2 * place + 1))
+            if 0 <= s + X_LEAD < TOKEN_TILES:
+                units.append(x_unit(s + X_LEAD))
+            return units
+
+        def transpose_and_copy(unit, second_copy):
+            sources = unit[0]
+            grouped = stage.tile([P, 4 * UNIT_COLS], BF16, name="grouped", align_bytes=64)
+            grouped_words = grouped[:].bitcast(F32).rearrange("p (b a r u) -> p b a r u", b=2, a=2, u=2)
+            for b in range(2):
+                bank = tpsum.tile([P, 2, 2, P], F32, name="bank")
+                for a in range(2):
+                    for u in range(2):
+                        nc.tensor.transpose(bank[:, a, u, :], sources[2 * b + a][:, u * P : (u + 1) * P], ident[:])
+                copy = nc.scalar.copy if b == 0 else second_copy
+                copy(out=grouped_words[:, b], in_=bank[:].rearrange("p a u r -> p a r u"))
+            return grouped
+
+        def quantise(unit, grouped):
+            nc.vector.quantize_mx(out=unit[1][:].bitcast(FP8X4), scales=unit[2][:], in_=grouped[:])
+
+        accs = {}
+        rms_of = {}
+        inv_of = {}
+
+        def multiply(i):
+            b, t = divmod(i, TOKEN_TILES)
+            acc = mpsum.tile([P, BLOCK_COLS], F32, name="acc")
+            for g in range(PASSES):
+                tokens = slice(g * P, (g + 1) * P)
+                nc.tensor.matmul_mx(
+                    out=acc[:],
+                    lhsT=x_codes[t][:, tokens].bitcast(FP8X4),
+                    lhsT_scale=x_scales[t][:, tokens],
+                    rhs=w_codes[b * PASSES + g][:].bitcast(FP8X4),
+                    rhs_scale=w_scales[b * PASSES + g][:],
+                    start=(g == 0),
+                    stop=(g == PASSES - 1),
+                )
+            accs[i] = acc
+
+        def root_mean_square(i):
+            acc = accs[i]
+            squares = work.tile([P, BLOCK_COLS], F32, name="squares")
+            sumsq = small.tile([P, BLOCK_HEADS], F32, name="sumsq")
+            for h in range(BLOCK_HEADS):
+                cols = slice(h * HEAD_DIM, (h + 1) * HEAD_DIM)
+                nc.scalar.activation(
+                    out=squares[:, cols], in_=acc[:, cols], func=ACT.Square, accum_out=sumsq[:, h : h + 1]
+                )
+            rms = small.tile([P, BLOCK_HEADS], F32, name="rms")
+            nc.scalar.activation(out=rms[:], in_=sumsq[:], func=ACT.Sqrt, bias=eps_sb[:], scale=1.0 / HEAD_DIM)
+            rms_of[i] = rms
+
+        def invert(i):
+            inv = small.tile([P, BLOCK_HEADS], F32, name="inv")
+            nc.vector.reciprocal(out=inv[:], in_=rms_of[i][:])
+            inv_of[i] = inv
+
+        def rotate_and_store(i):
+            b, t = divmod(i, TOKEN_TILES)
+            pairs = accs[i][:].rearrange("p (h j e) -> p h j e", h=BLOCK_HEADS, e=2)
+            inv = inv_of[i]
+            from_even = work.tile([P, BLOCK_HEADS, PAIRS, 2], F32, name="from_even")
+            from_odd = work.tile([P, BLOCK_HEADS, PAIRS, 2], F32, name="from_odd")
+            for h in range(BLOCK_HEADS):
+                nc.vector.scalar_tensor_tensor(
+                    out=from_even[:, h],
+                    in0=pairs[:, h, :, 0:1].to_broadcast([P, PAIRS, 2]),
+                    scalar=inv[:, h : h + 1],
+                    in1=even_table[:, t],
+                    op0=ALU.mult,
+                    op1=ALU.mult,
+                )
+                nc.vector.scalar_tensor_tensor(
+                    out=from_odd[:, h],
+                    in0=pairs[:, h, :, 1:2].to_broadcast([P, PAIRS, 2]),
+                    scalar=inv[:, h : h + 1],
+                    in1=odd_table[:, t],
+                    op0=ALU.mult,
+                    op1=ALU.mult,
+                )
+            nc.gpsimd.tensor_tensor(out=from_even[:], in0=from_even[:], in1=from_odd[:], op=ALU.add)
+            nc.sync.dma_start(
+                out=out_view[:, t, b * BLOCK_COLS : (b + 1) * BLOCK_COLS],
+                in_=from_even[:].rearrange("p h j e -> p (h j e)"),
+            )
+
+        copied = []
+        for s in range(-W_LEAD, GROUPS + 2):
+            for unit, grouped in copied:
+                quantise(unit, grouped)
+            if 0 <= s - 1 < GROUPS:
+                root_mean_square(s - 1)
+            second_copy = nc.vector.tensor_copy if s < 0 else nc.scalar.copy
+            copied = [(unit, transpose_and_copy(unit, second_copy)) for unit in units_of_slot(s)]
+            if 0 <= s < GROUPS:
+                multiply(s)
+            if 0 <= s - 2 < GROUPS:
+                rotate_and_store(s - 2)
+            if 0 <= s - 1 < GROUPS:
+                invert(s - 1)

@@ -29,8 +29,9 @@ BLOCKS = HEADS // BLOCK_HEADS
 GROUPS = BLOCKS * TOKEN_TILES
 UNIT_COLS = 512
 
-W_LEAD = 3
+W_LEAD = 5
 X_LEAD = 2
+LOAD_LEAD = 8
 
 FLOPS = 2 * TOKENS * K * HEADS * HEAD_DIM
 
@@ -49,26 +50,14 @@ def tile_mla_pb_kernel(tc, x, wq, q_norm_w, freqs_cos, freqs_sin, out):
         keep = ctx.enter_context(tc.tile_pool(name="keep", bufs=1))
         stage = ctx.enter_context(tc.tile_pool(name="stage", bufs=4))
         work = ctx.enter_context(tc.tile_pool(name="work", bufs=3))
+        result = ctx.enter_context(tc.tile_pool(name="result", bufs=6))
         small = ctx.enter_context(tc.tile_pool(name="small", bufs=4))
         tpsum = ctx.enter_context(tc.psum_pool(name="tpsum", bufs=4))
         mpsum = ctx.enter_context(tc.psum_pool(name="mpsum", bufs=4))
         ctx.enter_context(tc.manual_schedule())
 
-        w_raw = [raw.tile([P, 2, K], BF16, name="w_raw%d" % i) for i in range(HEADS // 2)]
-        x_raw = [raw.tile([P, 2, K], BF16, name="x_raw%d" % i) for i in range(TOKEN_TILES // 2)]
-
-        def load_w(i):
-            nc.sync.dma_start(out=w_raw[i][:], in_=wq_view[:, 2 * i : 2 * i + 2, :])
-
-        def load_x(i):
-            nc.sync.dma_start(out=x_raw[i][:], in_=x_view[:, 2 * i : 2 * i + 2, :])
-
-        for i in range(BLOCK_HEADS // 2):
-            load_w(i)
-        for i in range(TOKEN_TILES // 2):
-            load_x(i)
-        for i in range(BLOCK_HEADS // 2, HEADS // 2):
-            load_w(i)
+        x_raw = [raw.tile([P, K], BF16, name="x_raw%d" % t) for t in range(TOKEN_TILES)]
+        w_raw = [raw.tile([P, BLOCK_HEADS, K_PASS], BF16, name="w_raw%d" % i) for i in range(BLOCKS * PASSES)]
 
         cos_sb = const.tile([P, TOKEN_TILES, PAIRS], BF16, name="cos_sb")
         sin_sb = const.tile([P, TOKEN_TILES, PAIRS], BF16, name="sin_sb")
@@ -81,68 +70,71 @@ def tile_mla_pb_kernel(tc, x, wq, q_norm_w, freqs_cos, freqs_sin, out):
 
         ident = const.tile([P, P], F32, name="ident")
         make_identity(nc, ident[:])
+        split_pairs = const.tile([P, P], F32, name="split_pairs")
+        nc.vector.tensor_copy(
+            out=split_pairs[:].rearrange("p (e j) -> p e j", e=2), in_=ident[:].rearrange("p (j e) -> p e j", e=2)
+        )
         eps_sb = const.tile([P, 1], F32, name="eps_sb")
         nc.vector.memset(eps_sb[:], EPS)
         warm = const.tile([P, 1], F32, name="warm")
-        nc.scalar.activation(out=warm[:], in_=eps_sb[:], func=ACT.Sqrt)
+        nc.scalar.activation(out=warm[:], in_=eps_sb[:], func=ACT.Abs_reciprocal_sqrt)
 
-        even_table = const.tile([P, TOKEN_TILES, PAIRS, 2], F32, name="even_table")
-        odd_table = const.tile([P, TOKEN_TILES, PAIRS, 2], F32, name="odd_table")
+        table = const.tile([P, TOKEN_TILES, 2, PAIRS, 2], F32, name="table")
         table_shape = [P, TOKEN_TILES, PAIRS]
         gain_even = gain_sb[:, :, 0].unsqueeze(1).to_broadcast(table_shape)
         gain_odd = gain_sb[:, :, 1].unsqueeze(1).to_broadcast(table_shape)
-        nc.vector.tensor_tensor(out=even_table[:, :, :, 0], in0=cos_sb[:], in1=gain_even, op=ALU.mult)
-        nc.vector.tensor_tensor(out=even_table[:, :, :, 1], in0=sin_sb[:], in1=gain_even, op=ALU.mult)
+        nc.vector.tensor_tensor(out=table[:, :, 0, :, 0], in0=cos_sb[:], in1=gain_even, op=ALU.mult)
+        nc.vector.tensor_tensor(out=table[:, :, 0, :, 1], in0=sin_sb[:], in1=gain_even, op=ALU.mult)
         nc.vector.scalar_tensor_tensor(
-            out=odd_table[:, :, :, 0], in0=sin_sb[:], scalar=-1.0, in1=gain_odd, op0=ALU.mult, op1=ALU.mult
+            out=table[:, :, 1, :, 0], in0=sin_sb[:], scalar=-1.0, in1=gain_odd, op0=ALU.mult, op1=ALU.mult
         )
-        nc.vector.tensor_tensor(out=odd_table[:, :, :, 1], in0=cos_sb[:], in1=gain_odd, op=ALU.mult)
+        nc.vector.tensor_tensor(out=table[:, :, 1, :, 1], in0=cos_sb[:], in1=gain_odd, op=ALU.mult)
 
         x_codes = [keep.tile([P, UNIT_COLS], U32, name="x_codes%d" % t, align_bytes=64) for t in range(TOKEN_TILES)]
         x_scales = [keep.tile([P, UNIT_COLS], U8, name="x_scales%d" % t, align_bytes=64) for t in range(TOKEN_TILES)]
         w_codes = [keep.tile([P, UNIT_COLS], U32, name="w_codes%d" % i, align_bytes=64) for i in range(BLOCKS * PASSES)]
         w_scales = [keep.tile([P, UNIT_COLS], U8, name="w_scales%d" % i, align_bytes=64) for i in range(BLOCKS * PASSES)]
 
-        def pass_words(rows, g):
-            return rows.bitcast(F32)[:, g * PASS_WORDS : (g + 1) * PASS_WORDS]
-
         def x_unit(t):
-            rows = x_raw[t // 2][:, t % 2, :]
-            return [pass_words(rows, g) for g in range(PASSES)], x_codes[t], x_scales[t]
+            words = x_raw[t][:].bitcast(F32)
+            sources = [words[:, g * PASS_WORDS : (g + 1) * PASS_WORDS] for g in range(PASSES)]
+            return x_view[:, t, :], x_raw[t], sources, x_codes[t], x_scales[t], ident
 
         def w_unit(b, g):
-            heads = [BLOCK_HEADS * b + a for a in range(BLOCK_HEADS)]
-            sources = [pass_words(w_raw[h // 2][:, h % 2, :], g) for h in heads]
-            return sources, w_codes[b * PASSES + g], w_scales[b * PASSES + g]
+            i = b * PASSES + g
+            rows = wq_view[:, b * BLOCK_HEADS : (b + 1) * BLOCK_HEADS, g * K_PASS : (g + 1) * K_PASS]
+            sources = [w_raw[i][:, a, :].bitcast(F32) for a in range(BLOCK_HEADS)]
+            return rows, w_raw[i], sources, w_codes[i], w_scales[i], split_pairs
 
         def units_of_slot(s):
             units = []
-            block, place = divmod(s + W_LEAD, TOKEN_TILES)
-            if block < BLOCKS and place < 2:
-                units.append(w_unit(block, 2 * place))
-                units.append(w_unit(block, 2 * place + 1))
+            block, g = divmod(s + W_LEAD, TOKEN_TILES)
+            if block < BLOCKS and g < PASSES:
+                units.append(w_unit(block, g))
             if 0 <= s + X_LEAD < TOKEN_TILES:
                 units.append(x_unit(s + X_LEAD))
             return units
 
+        def load(unit):
+            nc.sync.dma_start(out=unit[1][:], in_=unit[0])
+
         def transpose_and_copy(unit, second_copy):
-            sources = unit[0]
+            sources = unit[2]
             grouped = stage.tile([P, 4 * UNIT_COLS], BF16, name="grouped", align_bytes=64)
             grouped_words = grouped[:].bitcast(F32).rearrange("p (b a r u) -> p b a r u", b=2, a=2, u=2)
             for b in range(2):
                 bank = tpsum.tile([P, 2, 2, P], F32, name="bank")
                 for a in range(2):
                     for u in range(2):
-                        nc.tensor.transpose(bank[:, a, u, :], sources[2 * b + a][:, u * P : (u + 1) * P], ident[:])
+                        nc.tensor.transpose(bank[:, a, u, :], sources[2 * b + a][:, u * P : (u + 1) * P], unit[5][:])
                 copy = nc.scalar.copy if b == 0 else second_copy
                 copy(out=grouped_words[:, b], in_=bank[:].rearrange("p a u r -> p a r u"))
             return grouped
 
         def quantise(unit, grouped):
-            nc.vector.quantize_mx(out=unit[1][:].bitcast(FP8X4), scales=unit[2][:], in_=grouped[:])
+            nc.vector.quantize_mx(out=unit[3][:].bitcast(FP8X4), scales=unit[4][:], in_=grouped[:])
 
         accs = {}
-        rms_of = {}
         inv_of = {}
 
         def multiply(i):
@@ -161,7 +153,7 @@ def tile_mla_pb_kernel(tc, x, wq, q_norm_w, freqs_cos, freqs_sin, out):
                 )
             accs[i] = acc
 
-        def root_mean_square(i):
+        def inverse_rms(i):
             acc = accs[i]
             squares = work.tile([P, BLOCK_COLS], F32, name="squares")
             sumsq = small.tile([P, BLOCK_HEADS], F32, name="sumsq")
@@ -170,55 +162,53 @@ def tile_mla_pb_kernel(tc, x, wq, q_norm_w, freqs_cos, freqs_sin, out):
                 nc.scalar.activation(
                     out=squares[:, cols], in_=acc[:, cols], func=ACT.Square, accum_out=sumsq[:, h : h + 1]
                 )
-            rms = small.tile([P, BLOCK_HEADS], F32, name="rms")
-            nc.scalar.activation(out=rms[:], in_=sumsq[:], func=ACT.Sqrt, bias=eps_sb[:], scale=1.0 / HEAD_DIM)
-            rms_of[i] = rms
-
-        def invert(i):
             inv = small.tile([P, BLOCK_HEADS], F32, name="inv")
-            nc.vector.reciprocal(out=inv[:], in_=rms_of[i][:])
+            nc.scalar.activation(
+                out=inv[:], in_=sumsq[:], func=ACT.Abs_reciprocal_sqrt, bias=eps_sb[:], scale=1.0 / HEAD_DIM
+            )
             inv_of[i] = inv
 
         def rotate_and_store(i):
             b, t = divmod(i, TOKEN_TILES)
-            pairs = accs[i][:].rearrange("p (h j e) -> p h j e", h=BLOCK_HEADS, e=2)
+            acc = accs[i]
             inv = inv_of[i]
-            from_even = work.tile([P, BLOCK_HEADS, PAIRS, 2], F32, name="from_even")
-            from_odd = work.tile([P, BLOCK_HEADS, PAIRS, 2], F32, name="from_odd")
+            products = work.tile([P, BLOCK_HEADS, 2, PAIRS, 2], F32, name="products")
             for h in range(BLOCK_HEADS):
                 nc.vector.scalar_tensor_tensor(
-                    out=from_even[:, h],
-                    in0=pairs[:, h, :, 0:1].to_broadcast([P, PAIRS, 2]),
+                    out=products[:, h].rearrange("p x j e -> p (x j) e"),
+                    in0=acc[:, h * HEAD_DIM : (h + 1) * HEAD_DIM].unsqueeze(2).to_broadcast([P, HEAD_DIM, 2]),
                     scalar=inv[:, h : h + 1],
-                    in1=even_table[:, t],
+                    in1=table[:, t].rearrange("p x j e -> p (x j) e"),
                     op0=ALU.mult,
                     op1=ALU.mult,
                 )
-                nc.vector.scalar_tensor_tensor(
-                    out=from_odd[:, h],
-                    in0=pairs[:, h, :, 1:2].to_broadcast([P, PAIRS, 2]),
-                    scalar=inv[:, h : h + 1],
-                    in1=odd_table[:, t],
-                    op0=ALU.mult,
-                    op1=ALU.mult,
-                )
-            nc.gpsimd.tensor_tensor(out=from_even[:], in0=from_even[:], in1=from_odd[:], op=ALU.add)
+            rotated = result.tile([P, BLOCK_HEADS, HEAD_DIM], F32, name="rotated")
+            nc.gpsimd.tensor_tensor(
+                out=rotated[:],
+                in0=products[:, :, 0].rearrange("p h j e -> p h (j e)"),
+                in1=products[:, :, 1].rearrange("p h j e -> p h (j e)"),
+                op=ALU.add,
+            )
             nc.sync.dma_start(
                 out=out_view[:, t, b * BLOCK_COLS : (b + 1) * BLOCK_COLS],
-                in_=from_even[:].rearrange("p h j e -> p (h j e)"),
+                in_=rotated[:].rearrange("p h d -> p (h d)"),
             )
 
+        first_slot = -W_LEAD
+        for s in range(first_slot, first_slot + LOAD_LEAD):
+            for unit in units_of_slot(s):
+                load(unit)
         copied = []
-        for s in range(-W_LEAD, GROUPS + 2):
+        for s in range(first_slot, GROUPS + 2):
+            for unit in units_of_slot(s + LOAD_LEAD):
+                load(unit)
             for unit, grouped in copied:
                 quantise(unit, grouped)
             if 0 <= s - 1 < GROUPS:
-                root_mean_square(s - 1)
+                inverse_rms(s - 1)
             second_copy = nc.vector.tensor_copy if s < 0 else nc.scalar.copy
             copied = [(unit, transpose_and_copy(unit, second_copy)) for unit in units_of_slot(s)]
             if 0 <= s < GROUPS:
                 multiply(s)
             if 0 <= s - 2 < GROUPS:
                 rotate_and_store(s - 2)
-            if 0 <= s - 1 < GROUPS:
-                invert(s - 1)

@@ -118,7 +118,7 @@ def tile_mla_pb_kernel(tc, x, wq, q_norm_w, freqs_cos, freqs_sin, out):
         def load(unit):
             nc.sync.dma_start(out=unit[1][:], in_=unit[0])
 
-        def transpose_and_copy(unit, second_copy):
+        def transpose_and_copy(unit):
             sources = unit[2]
             grouped = stage.tile([P, 4 * UNIT_COLS], BF16, name="grouped", align_bytes=64)
             grouped_words = grouped[:].bitcast(F32).rearrange("p (b a r u) -> p b a r u", b=2, a=2, u=2)
@@ -127,14 +127,14 @@ def tile_mla_pb_kernel(tc, x, wq, q_norm_w, freqs_cos, freqs_sin, out):
                 for a in range(2):
                     for u in range(2):
                         nc.tensor.transpose(bank[:, a, u, :], sources[2 * b + a][:, u * P : (u + 1) * P], unit[5][:])
-                copy = nc.scalar.copy if b == 0 else second_copy
-                copy(out=grouped_words[:, b], in_=bank[:].rearrange("p a u r -> p a r u"))
+                nc.scalar.copy(out=grouped_words[:, b], in_=bank[:].rearrange("p a u r -> p a r u"))
             return grouped
 
         def quantise(unit, grouped):
             nc.vector.quantize_mx(out=unit[3][:].bitcast(FP8X4), scales=unit[4][:], in_=grouped[:])
 
         accs = {}
+        sumsq_of = {}
         inv_of = {}
 
         def multiply(i):
@@ -153,7 +153,7 @@ def tile_mla_pb_kernel(tc, x, wq, q_norm_w, freqs_cos, freqs_sin, out):
                 )
             accs[i] = acc
 
-        def inverse_rms(i):
+        def sum_squares(i):
             acc = accs[i]
             squares = work.tile([P, BLOCK_COLS], F32, name="squares")
             sumsq = small.tile([P, BLOCK_HEADS], F32, name="sumsq")
@@ -162,9 +162,12 @@ def tile_mla_pb_kernel(tc, x, wq, q_norm_w, freqs_cos, freqs_sin, out):
                 nc.scalar.activation(
                     out=squares[:, cols], in_=acc[:, cols], func=ACT.Square, accum_out=sumsq[:, h : h + 1]
                 )
+            sumsq_of[i] = sumsq
+
+        def inverse_rms(i):
             inv = small.tile([P, BLOCK_HEADS], F32, name="inv")
             nc.scalar.activation(
-                out=inv[:], in_=sumsq[:], func=ACT.Abs_reciprocal_sqrt, bias=eps_sb[:], scale=1.0 / HEAD_DIM
+                out=inv[:], in_=sumsq_of[i][:], func=ACT.Abs_reciprocal_sqrt, bias=eps_sb[:], scale=1.0 / HEAD_DIM
             )
             inv_of[i] = inv
 
@@ -205,9 +208,10 @@ def tile_mla_pb_kernel(tc, x, wq, q_norm_w, freqs_cos, freqs_sin, out):
             for unit, grouped in copied:
                 quantise(unit, grouped)
             if 0 <= s - 1 < GROUPS:
+                sum_squares(s - 1)
+            copied = [(unit, transpose_and_copy(unit)) for unit in units_of_slot(s)]
+            if 0 <= s - 1 < GROUPS:
                 inverse_rms(s - 1)
-            second_copy = nc.vector.tensor_copy if s < 0 else nc.scalar.copy
-            copied = [(unit, transpose_and_copy(unit, second_copy)) for unit in units_of_slot(s)]
             if 0 <= s < GROUPS:
                 multiply(s)
             if 0 <= s - 2 < GROUPS:

@@ -134,6 +134,7 @@ def tile_mla_pb_kernel(tc, x, wq, q_norm_w, freqs_cos, freqs_sin, out):
             nc.vector.quantize_mx(out=unit[3][:].bitcast(FP8X4), scales=unit[4][:], in_=grouped[:])
 
         accs = {}
+        squares_of = {}
         sumsq_of = {}
         inv_of = {}
 
@@ -153,16 +154,18 @@ def tile_mla_pb_kernel(tc, x, wq, q_norm_w, freqs_cos, freqs_sin, out):
                 )
             accs[i] = acc
 
-        def sum_squares(i):
-            acc = accs[i]
-            squares = work.tile([P, BLOCK_COLS], F32, name="squares")
-            sumsq = small.tile([P, BLOCK_HEADS], F32, name="sumsq")
-            for h in range(BLOCK_HEADS):
+        def sum_squares(i, heads):
+            if i not in sumsq_of:
+                squares_of[i] = work.tile([P, BLOCK_COLS], F32, name="squares")
+                sumsq_of[i] = small.tile([P, BLOCK_HEADS], F32, name="sumsq")
+            for h in heads:
                 cols = slice(h * HEAD_DIM, (h + 1) * HEAD_DIM)
                 nc.scalar.activation(
-                    out=squares[:, cols], in_=acc[:, cols], func=ACT.Square, accum_out=sumsq[:, h : h + 1]
+                    out=squares_of[i][:, cols],
+                    in_=accs[i][:, cols],
+                    func=ACT.Square,
+                    accum_out=sumsq_of[i][:, h : h + 1],
                 )
-            sumsq_of[i] = sumsq
 
         def inverse_rms(i):
             inv = small.tile([P, BLOCK_HEADS], F32, name="inv")
@@ -208,10 +211,12 @@ def tile_mla_pb_kernel(tc, x, wq, q_norm_w, freqs_cos, freqs_sin, out):
             for unit, grouped in copied:
                 quantise(unit, grouped)
             if 0 <= s - 1 < GROUPS:
-                sum_squares(s - 1)
-            copied = [(unit, transpose_and_copy(unit)) for unit in units_of_slot(s)]
+                sum_squares(s - 1, range(0, 1))
+            if 0 <= s - 2 < GROUPS:
+                inverse_rms(s - 2)
             if 0 <= s - 1 < GROUPS:
-                inverse_rms(s - 1)
+                sum_squares(s - 1, range(1, BLOCK_HEADS))
+            copied = [(unit, transpose_and_copy(unit)) for unit in units_of_slot(s)]
             if 0 <= s < GROUPS:
                 multiply(s)
             if 0 <= s - 2 < GROUPS:

@@ -61,12 +61,11 @@ def tile_mla_pb_kernel(tc, x, wq, q_norm_w, freqs_cos, freqs_sin, out):
 
         cos_sb = const.tile([P, TOKEN_TILES, PAIRS], BF16, name="cos_sb")
         sin_sb = const.tile([P, TOKEN_TILES, PAIRS], BF16, name="sin_sb")
-        gain_sb = const.tile([P, PAIRS, 2], BF16, name="gain_sb")
+        gain_rows = const.tile([P, HEAD_DIM], BF16, name="gain_rows")
+        nc.vector.memset(gain_rows[:], 0.0)
+        nc.scalar.dma_start(out=gain_rows[0:1, :], in_=q_norm_w.unsqueeze(0))
         nc.scalar.dma_start(out=cos_sb[:], in_=cos_view)
         nc.scalar.dma_start(out=sin_sb[:], in_=sin_view)
-        nc.scalar.dma_start(
-            out=gain_sb[:].rearrange("p j e -> p (j e)"), in_=q_norm_w.partition_broadcast(P)
-        )
 
         ident = const.tile([P, P], F32, name="ident")
         make_identity(nc, ident[:])
@@ -79,16 +78,28 @@ def tile_mla_pb_kernel(tc, x, wq, q_norm_w, freqs_cos, freqs_sin, out):
         warm = const.tile([P, 1], F32, name="warm")
         nc.scalar.activation(out=warm[:], in_=eps_sb[:], func=ACT.Abs_reciprocal_sqrt)
 
+        ones = const.tile([P, P], BF16, name="ones")
+        nc.vector.memset(ones[:], 1.0)
+
         table = const.tile([P, TOKEN_TILES, 2, PAIRS, 2], F32, name="table")
-        table_shape = [P, TOKEN_TILES, PAIRS]
-        gain_even = gain_sb[:, :, 0].unsqueeze(1).to_broadcast(table_shape)
-        gain_odd = gain_sb[:, :, 1].unsqueeze(1).to_broadcast(table_shape)
-        nc.vector.tensor_tensor(out=table[:, :, 0, :, 0], in0=cos_sb[:], in1=gain_even, op=ALU.mult)
-        nc.vector.tensor_tensor(out=table[:, :, 0, :, 1], in0=sin_sb[:], in1=gain_even, op=ALU.mult)
-        nc.vector.scalar_tensor_tensor(
-            out=table[:, :, 1, :, 0], in0=sin_sb[:], scalar=-1.0, in1=gain_odd, op0=ALU.mult, op1=ALU.mult
-        )
-        nc.vector.tensor_tensor(out=table[:, :, 1, :, 1], in0=cos_sb[:], in1=gain_odd, op=ALU.mult)
+
+        def build_table():
+            gain_ps = tpsum.tile([P, PAIRS, 2], F32, name="gain_ps", tag="bank")
+            nc.tensor.matmul(
+                out=gain_ps[:].rearrange("p j e -> p (j e)"), lhsT=ones[:], rhs=gain_rows[:], start=True, stop=True
+            )
+            gain_sb = const.tile([P, PAIRS, 2], F32, name="gain_sb")
+            minus_gain = const.tile([P, PAIRS, 2], F32, name="minus_gain")
+            nc.scalar.copy(out=gain_sb[:], in_=gain_ps[:])
+            nc.scalar.mul(out=minus_gain[:], in_=gain_ps[:], mul=-1.0)
+            table_shape = [P, TOKEN_TILES, PAIRS]
+            gain_even = gain_sb[:, :, 0].unsqueeze(1).to_broadcast(table_shape)
+            gain_odd = gain_sb[:, :, 1].unsqueeze(1).to_broadcast(table_shape)
+            minus_gain_odd = minus_gain[:, :, 1].unsqueeze(1).to_broadcast(table_shape)
+            nc.gpsimd.tensor_tensor(out=table[:, :, 0, :, 0], in0=cos_sb[:], in1=gain_even, op=ALU.mult)
+            nc.gpsimd.tensor_tensor(out=table[:, :, 0, :, 1], in0=sin_sb[:], in1=gain_even, op=ALU.mult)
+            nc.gpsimd.tensor_tensor(out=table[:, :, 1, :, 0], in0=sin_sb[:], in1=minus_gain_odd, op=ALU.mult)
+            nc.gpsimd.tensor_tensor(out=table[:, :, 1, :, 1], in0=cos_sb[:], in1=gain_odd, op=ALU.mult)
 
         x_codes = [keep.tile([P, UNIT_COLS], U32, name="x_codes%d" % t, align_bytes=64) for t in range(TOKEN_TILES)]
         x_scales = [keep.tile([P, UNIT_COLS], U8, name="x_scales%d" % t, align_bytes=64) for t in range(TOKEN_TILES)]
@@ -189,7 +200,8 @@ def tile_mla_pb_kernel(tc, x, wq, q_norm_w, freqs_cos, freqs_sin, out):
                     op1=ALU.mult,
                 )
             rotated = result.tile([P, BLOCK_HEADS, HEAD_DIM], F32, name="rotated")
-            nc.gpsimd.tensor_tensor(
+            adder = nc.vector if i == GROUPS - 1 else nc.gpsimd
+            adder.tensor_tensor(
                 out=rotated[:],
                 in0=products[:, :, 0].rearrange("p h j e -> p h (j e)"),
                 in1=products[:, :, 1].rearrange("p h j e -> p h (j e)"),
@@ -217,6 +229,8 @@ def tile_mla_pb_kernel(tc, x, wq, q_norm_w, freqs_cos, freqs_sin, out):
             if 0 <= s - 1 < GROUPS:
                 sum_squares(s - 1, range(1, BLOCK_HEADS))
             copied = [(unit, transpose_and_copy(unit)) for unit in units_of_slot(s)]
+            if s == first_slot + 1:
+                build_table()
             if 0 <= s < GROUPS:
                 multiply(s)
             if 0 <= s - 2 < GROUPS:

@@ -54,7 +54,6 @@ def tile_mla_pb_kernel(tc, x, wq, q_norm_w, freqs_cos, freqs_sin, out):
         small = ctx.enter_context(tc.tile_pool(name="small", bufs=4))
         tpsum = ctx.enter_context(tc.psum_pool(name="tpsum", bufs=4))
         mpsum = ctx.enter_context(tc.psum_pool(name="mpsum", bufs=4))
-        ctx.enter_context(tc.manual_schedule())
 
         x_raw = [raw.tile([P, K], BF16, name="x_raw%d" % t) for t in range(TOKEN_TILES)]
         w_raw = [raw.tile([P, BLOCK_HEADS, K_PASS], BF16, name="w_raw%d" % i) for i in range(BLOCKS * PASSES)]

from contextlib import ExitStack

import concourse.mybir as mybir
from concourse.masks import make_identity

FP8X4 = mybir.dt.float8_e4m3fn_x4
BF16 = mybir.dt.bfloat16
F32 = mybir.dt.float32
U32 = mybir.dt.uint32
U8 = mybir.dt.uint8
ACT = mybir.ActivationFunctionType
ALU = mybir.AluOpType

P = 128
TOKENS = 1024
K = 2048
HEADS = 16
HEAD_DIM = 128
PAIRS = HEAD_DIM // 2
EPS = 1e-6

K_PASS = 4 * P
PASSES = K // K_PASS
PASS_WORDS = K_PASS // 2
TOKEN_TILES = TOKENS // P
BLOCK_HEADS = 4
BLOCK_COLS = BLOCK_HEADS * HEAD_DIM
BLOCKS = HEADS // BLOCK_HEADS
GROUPS = BLOCKS * TOKEN_TILES
UNIT_COLS = 512

W_LEAD = 5
X_LEAD = 2
LOAD_LEAD = 8

FLOPS = 2 * TOKENS * K * HEADS * HEAD_DIM


def tile_mla_pb_kernel(tc, x, wq, q_norm_w, freqs_cos, freqs_sin, out):
    nc = tc.nc
    x_view = x.rearrange("b (p t) k -> p (b t) k", t=TOKEN_TILES)
    cos_view = freqs_cos.rearrange("(p t) j -> p t j", t=TOKEN_TILES)
    sin_view = freqs_sin.rearrange("(p t) j -> p t j", t=TOKEN_TILES)
    out_view = out.rearrange("b (p t) h d -> p (b t) (h d)", t=TOKEN_TILES)
    wq_view = wq.rearrange("(h p) k -> p h k", p=P)

    with ExitStack() as ctx:
        const = ctx.enter_context(tc.tile_pool(name="const", bufs=1))
        raw = ctx.enter_context(tc.tile_pool(name="raw", bufs=1))
        keep = ctx.enter_context(tc.tile_pool(name="keep", bufs=1))
        stage = ctx.enter_context(tc.tile_pool(name="stage", bufs=4))
        work = ctx.enter_context(tc.tile_pool(name="work", bufs=3))
        result = ctx.enter_context(tc.tile_pool(name="result", bufs=6))
        small = ctx.enter_context(tc.tile_pool(name="small", bufs=4))
        tpsum = ctx.enter_context(tc.psum_pool(name="tpsum", bufs=4))
        mpsum = ctx.enter_context(tc.psum_pool(name="mpsum", bufs=4))

        x_raw = [raw.tile([P, K], BF16, name="x_raw%d" % t) for t in range(TOKEN_TILES)]
        w_raw = [raw.tile([P, BLOCK_HEADS, K_PASS], BF16, name="w_raw%d" % i) for i in range(BLOCKS * PASSES)]

        cos_sb = const.tile([P, TOKEN_TILES, PAIRS], BF16, name="cos_sb")
        sin_sb = const.tile([P, TOKEN_TILES, PAIRS], BF16, name="sin_sb")
        gain_rows = const.tile([P, HEAD_DIM], BF16, name="gain_rows")
        nc.vector.memset(gain_rows[:], 0.0)
        nc.scalar.dma_start(out=gain_rows[0:1, :], in_=q_norm_w.unsqueeze(0))
        nc.scalar.dma_start(out=cos_sb[:], in_=cos_view)
        nc.scalar.dma_start(out=sin_sb[:], in_=sin_view)

        ident = const.tile([P, P], F32, name="ident")
        make_identity(nc, ident[:])
        split_pairs = const.tile([P, P], F32, name="split_pairs")
        nc.vector.tensor_copy(
            out=split_pairs[:].rearrange("p (e j) -> p e j", e=2), in_=ident[:].rearrange("p (j e) -> p e j", e=2)
        )
        eps_sb = const.tile([P, 1], F32, name="eps_sb")
        nc.vector.memset(eps_sb[:], EPS)
        warm = const.tile([P, 1], F32, name="warm")
        nc.scalar.activation(out=warm[:], in_=eps_sb[:], func=ACT.Abs_reciprocal_sqrt)

        ones = const.tile([P, P], BF16, name="ones")
        nc.vector.memset(ones[:], 1.0)

        table = const.tile([P, TOKEN_TILES, 2, PAIRS, 2], F32, name="table")

        def build_table():
            gain_ps = tpsum.tile([P, PAIRS, 2], F32, name="gain_ps", tag="bank")
            nc.tensor.matmul(
                out=gain_ps[:].rearrange("p j e -> p (j e)"), lhsT=ones[:], rhs=gain_rows[:], start=True, stop=True
            )
            gain_sb = const.tile([P, PAIRS, 2], F32, name="gain_sb")
            minus_gain = const.tile([P, PAIRS, 2], F32, name="minus_gain")
            nc.scalar.copy(out=gain_sb[:], in_=gain_ps[:])
            nc.scalar.mul(out=minus_gain[:], in_=gain_ps[:], mul=-1.0)
            table_shape = [P, TOKEN_TILES, PAIRS]
            gain_even = gain_sb[:, :, 0].unsqueeze(1).to_broadcast(table_shape)
            gain_odd = gain_sb[:, :, 1].unsqueeze(1).to_broadcast(table_shape)
            minus_gain_odd = minus_gain[:, :, 1].unsqueeze(1).to_broadcast(table_shape)
            nc.gpsimd.tensor_tensor(out=table[:, :, 0, :, 0], in0=cos_sb[:], in1=gain_even, op=ALU.mult)
            nc.gpsimd.tensor_tensor(out=table[:, :, 0, :, 1], in0=sin_sb[:], in1=gain_even, op=ALU.mult)
            nc.gpsimd.tensor_tensor(out=table[:, :, 1, :, 0], in0=sin_sb[:], in1=minus_gain_odd, op=ALU.mult)
            nc.gpsimd.tensor_tensor(out=table[:, :, 1, :, 1], in0=cos_sb[:], in1=gain_odd, op=ALU.mult)

        x_codes = [keep.tile([P, UNIT_COLS], U32, name="x_codes%d" % t, align_bytes=64) for t in range(TOKEN_TILES)]
        x_scales = [keep.tile([P, UNIT_COLS], U8, name="x_scales%d" % t, align_bytes=64) for t in range(TOKEN_TILES)]
        w_codes = [keep.tile([P, UNIT_COLS], U32, name="w_codes%d" % i, align_bytes=64) for i in range(BLOCKS * PASSES)]
        w_scales = [keep.tile([P, UNIT_COLS], U8, name="w_scales%d" % i, align_bytes=64) for i in range(BLOCKS * PASSES)]

        def x_unit(t):
            words = x_raw[t][:].bitcast(F32)
            sources = [words[:, g * PASS_WORDS : (g + 1) * PASS_WORDS] for g in range(PASSES)]
            return x_view[:, t, :], x_raw[t], sources, x_codes[t], x_scales[t], ident

        def w_unit(b, g):
            i = b * PASSES + g
            rows = wq_view[:, b * BLOCK_HEADS : (b + 1) * BLOCK_HEADS, g * K_PASS : (g + 1) * K_PASS]
            sources = [w_raw[i][:, a, :].bitcast(F32) for a in range(BLOCK_HEADS)]
            return rows, w_raw[i], sources, w_codes[i], w_scales[i], split_pairs

        def units_of_slot(s):
            units = []
            block, g = divmod(s + W_LEAD, TOKEN_TILES)
            if block < BLOCKS and g < PASSES:
                units.append(w_unit(block, g))
            if 0 <= s + X_LEAD < TOKEN_TILES:
                units.append(x_unit(s + X_LEAD))
            return units

        def load(unit):
            nc.sync.dma_start(out=unit[1][:], in_=unit[0])

        def transpose_and_copy(unit):
            sources = unit[2]
            grouped = stage.tile([P, 4 * UNIT_COLS], BF16, name="grouped", align_bytes=64)
            grouped_words = grouped[:].bitcast(F32).rearrange("p (b a r u) -> p b a r u", b=2, a=2, u=2)
            for b in range(2):
                bank = tpsum.tile([P, 2, 2, P], F32, name="bank")
                for a in range(2):
                    for u in range(2):
                        nc.tensor.transpose(bank[:, a, u, :], sources[2 * b + a][:, u * P : (u + 1) * P], unit[5][:])
                nc.scalar.copy(out=grouped_words[:, b], in_=bank[:].rearrange("p a u r -> p a r u"))
            return grouped

        def quantise(unit, grouped):
            nc.vector.quantize_mx(out=unit[3][:].bitcast(FP8X4), scales=unit[4][:], in_=grouped[:])

        accs = {}
        squares_of = {}
        sumsq_of = {}
        inv_of = {}

        def multiply(i):
            b, t = divmod(i, TOKEN_TILES)
            acc = mpsum.tile([P, BLOCK_COLS], F32, name="acc")
            for g in range(PASSES):
                tokens = slice(g * P, (g + 1) * P)
                nc.tensor.matmul_mx(
                    out=acc[:],
                    lhsT=x_codes[t][:, tokens].bitcast(FP8X4),
                    lhsT_scale=x_scales[t][:, tokens],
                    rhs=w_codes[b * PASSES + g][:].bitcast(FP8X4),
                    rhs_scale=w_scales[b * PASSES + g][:],
                    start=(g == 0),
                    stop=(g == PASSES - 1),
                )
            accs[i] = acc

        def sum_squares(i, heads):
            if i not in sumsq_of:
                squares_of[i] = work.tile([P, BLOCK_COLS], F32, name="squares")
                sumsq_of[i] = small.tile([P, BLOCK_HEADS], F32, name="sumsq")
            for h in heads:
                cols = slice(h * HEAD_DIM, (h + 1) * HEAD_DIM)
                nc.scalar.activation(
                    out=squares_of[i][:, cols],
                    in_=accs[i][:, cols],
                    func=ACT.Square,
                    accum_out=sumsq_of[i][:, h : h + 1],
                )

        def inverse_rms(i):
            inv = small.tile([P, BLOCK_HEADS], F32, name="inv")
            nc.scalar.activation(
                out=inv[:], in_=sumsq_of[i][:], func=ACT.Abs_reciprocal_sqrt, bias=eps_sb[:], scale=1.0 / HEAD_DIM
            )
            inv_of[i] = inv

        def rotate_and_store(i):
            b, t = divmod(i, TOKEN_TILES)
            acc = accs[i]
            inv = inv_of[i]
            products = work.tile([P, BLOCK_HEADS, 2, PAIRS, 2], F32, name="products")
            for h in range(BLOCK_HEADS):
                nc.vector.scalar_tensor_tensor(
                    out=products[:, h].rearrange("p x j e -> p (x j) e"),
                    in0=acc[:, h * HEAD_DIM : (h + 1) * HEAD_DIM].unsqueeze(2).to_broadcast([P, HEAD_DIM, 2]),
                    scalar=inv[:, h : h + 1],
                    in1=table[:, t].rearrange("p x j e -> p (x j) e"),
                    op0=ALU.mult,
                    op1=ALU.mult,
                )
            rotated = result.tile([P, BLOCK_HEADS, HEAD_DIM], F32, name="rotated")
            adder = nc.vector if i == GROUPS - 1 else nc.gpsimd
            adder.tensor_tensor(
                out=rotated[:],
                in0=products[:, :, 0].rearrange("p h j e -> p h (j e)"),
                in1=products[:, :, 1].rearrange("p h j e -> p h (j e)"),
                op=ALU.add,
            )
            nc.sync.dma_start(
                out=out_view[:, t, b * BLOCK_COLS : (b + 1) * BLOCK_COLS],
                in_=rotated[:].rearrange("p h d -> p (h d)"),
            )

        first_slot = -W_LEAD
        for s in range(first_slot, first_slot + LOAD_LEAD):
            for unit in units_of_slot(s):
                load(unit)
        copied = []
        for s in range(first_slot, GROUPS + 2):
            for unit in units_of_slot(s + LOAD_LEAD):
                load(unit)
            for unit, grouped in copied:
                quantise(unit, grouped)
            if 0 <= s - 1 < GROUPS:
                sum_squares(s - 1, range(0, 1))
            if 0 <= s - 2 < GROUPS:
                inverse_rms(s - 2)
            if 0 <= s - 1 < GROUPS:
                sum_squares(s - 1, range(1, BLOCK_HEADS))
            copied = [(unit, transpose_and_copy(unit)) for unit in units_of_slot(s)]
            if s == first_slot + 1:
                build_table()
            if 0 <= s < GROUPS:
                multiply(s)
            if 0 <= s - 2 < GROUPS:
                rotate_and_store(s - 2)
